import numpy as np
import ml_dtypes

BF16 = ml_dtypes.bfloat16


def bf(x):
    return np.asarray(x, np.float32).astype(BF16)


def f32(x):
    return np.asarray(x, np.float32)


def f64(x):
    return np.asarray(x).astype(np.float64)


def striped(idx):
    return np.tile(idx.reshape(-1, 16).T, (8, 1))


C, S, N, A = 512, 512, 64, 4
LO = 0.02


def logp(shape):
    return f32(np.log(np.random.uniform(LO, 1.0, shape)))


def setup_inputs():
    z = np.random.standard_normal((A, N))
    lw = z - np.log(np.exp(z).sum(axis=0, keepdims=True))
    return {"base": logp((C, S)), "left": logp((C, A * N)), "right": logp((C, A * N)), "logw": f32(lw.reshape(1, A * N)), "offs": striped(np.random.permutation(S)[:N])}


def reference(base, left, right, logw, offs):
    idx = offs[:16].T.reshape(-1)
    t = (f64(left) + f64(right) + f64(logw)).reshape(C, A, N)
    m = t.max(axis=1)
    s = np.exp(t - m[:, None, :]).sum(axis=1)
    out = f64(base).copy()
    out[:, idx] = m + np.log(s)
    return out

@@ -1,0 +1,71 @@
+import concourse.mybir as mybir
+
+F32 = mybir.dt.float32
+U16 = mybir.dt.uint16
+ADD = mybir.AluOpType.add
+SUBTRACT = mybir.AluOpType.subtract
+MAX = mybir.AluOpType.max
+EXP = mybir.ActivationFunctionType.Exp
+LN = mybir.ActivationFunctionType.Ln
+
+P = 128
+SAMPLES = 512
+PLACES = 512
+NODES = 64
+CHILDREN = 4
+ELEMENTS = CHILDREN * NODES
+BLOCKS = SAMPLES // P
+
+
+def tile_tensorcircuit_kernel(tc, base, left, right, logw, offs, out):
+    nc = tc.nc
+    with (
+        tc.tile_pool(name="held", bufs=1) as held,
+        tc.tile_pool(name="work", bufs=BLOCKS) as work,
+    ):
+        lefts = [held.tile([P, ELEMENTS], F32, name=f"left{b}") for b in range(BLOCKS)]
+        rights = [held.tile([P, ELEMENTS], F32, name=f"right{b}") for b in range(BLOCKS)]
+        windows = [held.tile([P, PLACES], F32, name=f"window{b}") for b in range(BLOCKS)]
+        logw_all = held.tile([P, ELEMENTS], F32, name="logw_all")
+        offsets = held.tile([P, NODES // 16], U16, name="offsets")
+
+        nc.sync.dma_start(lefts[0][:], left[0:P, :])
+        nc.sync.dma_start(rights[0][:], right[0:P, :])
+        nc.sync.dma_start(logw_all[:], logw.to_broadcast([P, ELEMENTS]))
+        for b in range(1, BLOCKS):
+            nc.sync.dma_start(lefts[b][:], left[b * P : (b + 1) * P, :])
+            nc.sync.dma_start(rights[b][:], right[b * P : (b + 1) * P, :])
+        nc.sync.dma_start(offsets[:], offs)
+        for b in range(BLOCKS):
+            nc.sync.dma_start(windows[b][:], base[b * P : (b + 1) * P, :])
+
+        for b in range(BLOCKS):
+            product = work.tile([P, ELEMENTS], F32, name="product")
+            nc.vector.tensor_tensor(product[:], lefts[b][:], rights[b][:], ADD)
+            t = work.tile([P, ELEMENTS], F32, name="t")
+            nc.vector.tensor_tensor(t[:], product[:], logw_all[:], ADD)
+
+            m_pair = work.tile([P, 2 * NODES], F32, name="m_pair")
+            nc.vector.tensor_tensor(m_pair[:], t[:, : 2 * NODES], t[:, 2 * NODES :], MAX)
+            m = work.tile([P, NODES], F32, name="m")
+            nc.vector.tensor_tensor(m[:], m_pair[:, :NODES], m_pair[:, NODES:], MAX)
+
+            shifted = work.tile([P, ELEMENTS], F32, name="shifted")
+            nc.vector.tensor_tensor(
+                shifted[:].rearrange("p (a j) -> p a j", a=CHILDREN),
+                t[:].rearrange("p (a j) -> p a j", a=CHILDREN),
+                m[:].unsqueeze(1).to_broadcast([P, CHILDREN, NODES]),
+                SUBTRACT,
+            )
+            e = work.tile([P, ELEMENTS], F32, name="e")
+            nc.scalar.activation(e[:], shifted[:], EXP)
+
+            s_pair = work.tile([P, 2 * NODES], F32, name="s_pair")
+            nc.vector.tensor_tensor(s_pair[:], e[:, : 2 * NODES], e[:, 2 * NODES :], ADD)
+            s = work.tile([P, NODES], F32, name="s")
+            nc.vector.tensor_tensor(s[:], s_pair[:, :NODES], s_pair[:, NODES:], ADD)
+            log_s = work.tile([P, NODES], F32, name="log_s")
+            nc.scalar.activation(log_s[:], s[:], LN)
+
+            nc.vector.tensor_tensor(windows[b][:].indirect(offsets[:]), m[:], log_s[:], ADD)
+            nc.sync.dma_start(out[b * P : (b + 1) * P, :], windows[b][:])

@@ -19,10 +19,7 @@ BLOCKS = SAMPLES // P
 
 def tile_tensorcircuit_kernel(tc, base, left, right, logw, offs, out):
     nc = tc.nc
-    with (
-        tc.tile_pool(name="held", bufs=1) as held,
-        tc.tile_pool(name="work", bufs=BLOCKS) as work,
-    ):
+    with tc.tile_pool(name="held", bufs=1) as held:
         lefts = [held.tile([P, ELEMENTS], F32, name=f"left{b}") for b in range(BLOCKS)]
         rights = [held.tile([P, ELEMENTS], F32, name=f"right{b}") for b in range(BLOCKS)]
         windows = [held.tile([P, PLACES], F32, name=f"window{b}") for b in range(BLOCKS)]
@@ -39,33 +36,38 @@ def tile_tensorcircuit_kernel(tc, base, left, right, logw, offs, out):
         for b in range(BLOCKS):
             nc.sync.dma_start(windows[b][:], base[b * P : (b + 1) * P, :])
 
+        maxima = [held.tile([P, NODES], F32, name=f"m{b}") for b in range(BLOCKS)]
+        sums = [held.tile([P, NODES], F32, name=f"s{b}") for b in range(BLOCKS)]
+
         for b in range(BLOCKS):
-            product = work.tile([P, ELEMENTS], F32, name="product")
+            m, s = maxima[b], sums[b]
+            product = held.tile([P, ELEMENTS], F32, name=f"product{b}")
             nc.vector.tensor_tensor(product[:], lefts[b][:], rights[b][:], ADD)
-            t = work.tile([P, ELEMENTS], F32, name="t")
+            t = held.tile([P, ELEMENTS], F32, name=f"t{b}")
             nc.vector.tensor_tensor(t[:], product[:], logw_all[:], ADD)
 
-            m_pair = work.tile([P, 2 * NODES], F32, name="m_pair")
+            m_pair = held.tile([P, 2 * NODES], F32, name=f"m_pair{b}")
             nc.vector.tensor_tensor(m_pair[:], t[:, : 2 * NODES], t[:, 2 * NODES :], MAX)
-            m = work.tile([P, NODES], F32, name="m")
             nc.vector.tensor_tensor(m[:], m_pair[:, :NODES], m_pair[:, NODES:], MAX)
 
-            shifted = work.tile([P, ELEMENTS], F32, name="shifted")
+            shifted = held.tile([P, ELEMENTS], F32, name=f"shifted{b}")
             nc.vector.tensor_tensor(
                 shifted[:].rearrange("p (a j) -> p a j", a=CHILDREN),
                 t[:].rearrange("p (a j) -> p a j", a=CHILDREN),
                 m[:].unsqueeze(1).to_broadcast([P, CHILDREN, NODES]),
                 SUBTRACT,
             )
-            e = work.tile([P, ELEMENTS], F32, name="e")
+            e = held.tile([P, ELEMENTS], F32, name=f"e{b}")
             nc.scalar.activation(e[:], shifted[:], EXP)
 
-            s_pair = work.tile([P, 2 * NODES], F32, name="s_pair")
+            s_pair = held.tile([P, 2 * NODES], F32, name=f"s_pair{b}")
             nc.vector.tensor_tensor(s_pair[:], e[:, : 2 * NODES], e[:, 2 * NODES :], ADD)
-            s = work.tile([P, NODES], F32, name="s")
             nc.vector.tensor_tensor(s[:], s_pair[:, :NODES], s_pair[:, NODES:], ADD)
-            log_s = work.tile([P, NODES], F32, name="log_s")
-            nc.scalar.activation(log_s[:], s[:], LN)
 
-            nc.vector.tensor_tensor(windows[b][:].indirect(offsets[:]), m[:], log_s[:], ADD)
+        for b in range(BLOCKS):
+            log_s = held.tile([P, NODES], F32, name=f"log_s{b}")
+            nc.scalar.activation(log_s[:], sums[b][:], LN)
+            nc.vector.tensor_tensor(
+                windows[b][:].indirect(offsets[:]), maxima[b][:], log_s[:], ADD
+            )
             nc.sync.dma_start(out[b * P : (b + 1) * P, :], windows[b][:])

@@ -15,59 +15,70 @@ NODES = 64
 CHILDREN = 4
 ELEMENTS = CHILDREN * NODES
 BLOCKS = SAMPLES // P
+GROUP = 2
+GROUPS = BLOCKS // GROUP
 
 
 def tile_tensorcircuit_kernel(tc, base, left, right, logw, offs, out):
     nc = tc.nc
+    left_blocks = left.rearrange("(p k) d -> p k d", k=BLOCKS)
+    right_blocks = right.rearrange("(p k) d -> p k d", k=BLOCKS)
+    base_blocks = base.rearrange("(p k) d -> k p d", k=BLOCKS)
+    out_blocks = out.rearrange("(p k) d -> k p d", k=BLOCKS)
+
     with tc.tile_pool(name="held", bufs=1) as held:
-        lefts = [held.tile([P, ELEMENTS], F32, name=f"left{b}") for b in range(BLOCKS)]
-        rights = [held.tile([P, ELEMENTS], F32, name=f"right{b}") for b in range(BLOCKS)]
-        windows = [held.tile([P, PLACES], F32, name=f"window{b}") for b in range(BLOCKS)]
+        lefts = [held.tile([P, GROUP, ELEMENTS], F32, name=f"left{g}") for g in range(GROUPS)]
+        rights = [held.tile([P, GROUP, ELEMENTS], F32, name=f"right{g}") for g in range(GROUPS)]
+        windows = [held.tile([P, PLACES], F32, name=f"window{k}") for k in range(BLOCKS)]
         logw_all = held.tile([P, ELEMENTS], F32, name="logw_all")
         offsets = held.tile([P, NODES // 16], U16, name="offsets")
 
-        nc.sync.dma_start(lefts[0][:], left[0:P, :])
-        nc.sync.dma_start(rights[0][:], right[0:P, :])
-        nc.sync.dma_start(logw_all[:], logw.to_broadcast([P, ELEMENTS]))
-        for b in range(1, BLOCKS):
-            nc.sync.dma_start(lefts[b][:], left[b * P : (b + 1) * P, :])
-            nc.sync.dma_start(rights[b][:], right[b * P : (b + 1) * P, :])
+        for g in range(GROUPS):
+            nc.sync.dma_start(lefts[g][:], left_blocks[:, g * GROUP : (g + 1) * GROUP, :])
+            nc.sync.dma_start(rights[g][:], right_blocks[:, g * GROUP : (g + 1) * GROUP, :])
+            if g == 0:
+                nc.sync.dma_start(logw_all[:], logw.to_broadcast([P, ELEMENTS]))
         nc.sync.dma_start(offsets[:], offs)
-        for b in range(BLOCKS):
-            nc.sync.dma_start(windows[b][:], base[b * P : (b + 1) * P, :])
+        for k in range(BLOCKS):
+            nc.sync.dma_start(windows[k][:], base_blocks[k])
 
-        maxima = [held.tile([P, NODES], F32, name=f"m{b}") for b in range(BLOCKS)]
-        sums = [held.tile([P, NODES], F32, name=f"s{b}") for b in range(BLOCKS)]
+        m_all = held.tile([P, BLOCKS, NODES], F32, name="m_all")
+        e_all = held.tile([P, BLOCKS, ELEMENTS], F32, name="e_all")
 
-        for b in range(BLOCKS):
-            m, s = maxima[b], sums[b]
-            product = held.tile([P, ELEMENTS], F32, name=f"product{b}")
-            nc.vector.tensor_tensor(product[:], lefts[b][:], rights[b][:], ADD)
-            t = held.tile([P, ELEMENTS], F32, name=f"t{b}")
-            nc.vector.tensor_tensor(t[:], product[:], logw_all[:], ADD)
-
-            m_pair = held.tile([P, 2 * NODES], F32, name=f"m_pair{b}")
-            nc.vector.tensor_tensor(m_pair[:], t[:, : 2 * NODES], t[:, 2 * NODES :], MAX)
-            nc.vector.tensor_tensor(m[:], m_pair[:, :NODES], m_pair[:, NODES:], MAX)
-
-            shifted = held.tile([P, ELEMENTS], F32, name=f"shifted{b}")
+        for g in range(GROUPS):
+            blocks = slice(g * GROUP, (g + 1) * GROUP)
+            product = held.tile([P, GROUP, ELEMENTS], F32, name=f"product{g}")
+            nc.vector.tensor_tensor(product[:], lefts[g][:], rights[g][:], ADD)
+            t = held.tile([P, GROUP, ELEMENTS], F32, name=f"t{g}")
             nc.vector.tensor_tensor(
-                shifted[:].rearrange("p (a j) -> p a j", a=CHILDREN),
-                t[:].rearrange("p (a j) -> p a j", a=CHILDREN),
-                m[:].unsqueeze(1).to_broadcast([P, CHILDREN, NODES]),
+                t[:], product[:], logw_all[:].unsqueeze(1).to_broadcast([P, GROUP, ELEMENTS]), ADD
+            )
+
+            m_pair = held.tile([P, GROUP, 2 * NODES], F32, name=f"m_pair{g}")
+            nc.vector.tensor_tensor(m_pair[:], t[:, :, : 2 * NODES], t[:, :, 2 * NODES :], MAX)
+            m = m_all[:, blocks, :]
+            nc.vector.tensor_tensor(m, m_pair[:, :, :NODES], m_pair[:, :, NODES:], MAX)
+
+            shifted = held.tile([P, GROUP, ELEMENTS], F32, name=f"shifted{g}")
+            nc.vector.tensor_tensor(
+                shifted[:].rearrange("p k (a j) -> p k a j", a=CHILDREN),
+                t[:].rearrange("p k (a j) -> p k a j", a=CHILDREN),
+                m.unsqueeze(2).to_broadcast([P, GROUP, CHILDREN, NODES]),
                 SUBTRACT,
             )
-            e = held.tile([P, ELEMENTS], F32, name=f"e{b}")
-            nc.scalar.activation(e[:], shifted[:], EXP)
+            nc.scalar.activation(e_all[:, blocks, :], shifted[:], EXP)
 
-            s_pair = held.tile([P, 2 * NODES], F32, name=f"s_pair{b}")
-            nc.vector.tensor_tensor(s_pair[:], e[:, : 2 * NODES], e[:, 2 * NODES :], ADD)
-            nc.vector.tensor_tensor(s[:], s_pair[:, :NODES], s_pair[:, NODES:], ADD)
+        s_pair_all = held.tile([P, BLOCKS, 2 * NODES], F32, name="s_pair_all")
+        nc.vector.tensor_tensor(
+            s_pair_all[:], e_all[:, :, : 2 * NODES], e_all[:, :, 2 * NODES :], ADD
+        )
+        s_all = held.tile([P, BLOCKS, NODES], F32, name="s_all")
+        nc.vector.tensor_tensor(s_all[:], s_pair_all[:, :, :NODES], s_pair_all[:, :, NODES:], ADD)
 
-        for b in range(BLOCKS):
-            log_s = held.tile([P, NODES], F32, name=f"log_s{b}")
-            nc.scalar.activation(log_s[:], sums[b][:], LN)
+        for k in range(BLOCKS):
+            log_s = held.tile([P, NODES], F32, name=f"log_s{k}")
+            nc.scalar.activation(log_s[:], s_all[:, k, :], LN)
             nc.vector.tensor_tensor(
-                windows[b][:].indirect(offsets[:]), maxima[b][:], log_s[:], ADD
+                windows[k][:].indirect(offsets[:]), m_all[:, k, :], log_s[:], ADD
             )
-            nc.sync.dma_start(out[b * P : (b + 1) * P, :], windows[b][:])
+            nc.sync.dma_start(out_blocks[k], windows[k][:])

@@ -33,26 +33,29 @@ def tile_tensorcircuit_kernel(tc, base, left, right, logw, offs, out):
         logw_all = held.tile([P, ELEMENTS], F32, name="logw_all")
         offsets = held.tile([P, NODES // 16], U16, name="offsets")
 
+        nc.sync.dma_start(logw_all[:], logw.to_broadcast([P, ELEMENTS]))
+        for g in range(GROUPS):
+            nc.sync.dma_start(rights[g][:], right_blocks[:, g * GROUP : (g + 1) * GROUP, :])
         for g in range(GROUPS):
             nc.sync.dma_start(lefts[g][:], left_blocks[:, g * GROUP : (g + 1) * GROUP, :])
-            nc.sync.dma_start(rights[g][:], right_blocks[:, g * GROUP : (g + 1) * GROUP, :])
-            if g == 0:
-                nc.sync.dma_start(logw_all[:], logw.to_broadcast([P, ELEMENTS]))
         nc.sync.dma_start(offsets[:], offs)
         for k in range(BLOCKS):
             nc.sync.dma_start(windows[k][:], base_blocks[k])
 
         m_all = held.tile([P, BLOCKS, NODES], F32, name="m_all")
-        e_all = held.tile([P, BLOCKS, ELEMENTS], F32, name="e_all")
+        s_pair_all = held.tile([P, BLOCKS, 2 * NODES], F32, name="s_pair_all")
 
         for g in range(GROUPS):
             blocks = slice(g * GROUP, (g + 1) * GROUP)
-            product = held.tile([P, GROUP, ELEMENTS], F32, name=f"product{g}")
-            nc.vector.tensor_tensor(product[:], lefts[g][:], rights[g][:], ADD)
-            t = held.tile([P, GROUP, ELEMENTS], F32, name=f"t{g}")
+            weighted = held.tile([P, GROUP, ELEMENTS], F32, name=f"weighted{g}")
             nc.vector.tensor_tensor(
-                t[:], product[:], logw_all[:].unsqueeze(1).to_broadcast([P, GROUP, ELEMENTS]), ADD
+                weighted[:],
+                rights[g][:],
+                logw_all[:].unsqueeze(1).to_broadcast([P, GROUP, ELEMENTS]),
+                ADD,
             )
+            t = held.tile([P, GROUP, ELEMENTS], F32, name=f"t{g}")
+            nc.vector.tensor_tensor(t[:], lefts[g][:], weighted[:], ADD)
 
             m_pair = held.tile([P, GROUP, 2 * NODES], F32, name=f"m_pair{g}")
             nc.vector.tensor_tensor(m_pair[:], t[:, :, : 2 * NODES], t[:, :, 2 * NODES :], MAX)
@@ -66,12 +69,13 @@ def tile_tensorcircuit_kernel(tc, base, left, right, logw, offs, out):
                 m.unsqueeze(2).to_broadcast([P, GROUP, CHILDREN, NODES]),
                 SUBTRACT,
             )
-            nc.scalar.activation(e_all[:, blocks, :], shifted[:], EXP)
+            e = held.tile([P, GROUP, ELEMENTS], F32, name=f"e{g}")
+            nc.scalar.activation(e[:], shifted[:], EXP)
 
-        s_pair_all = held.tile([P, BLOCKS, 2 * NODES], F32, name="s_pair_all")
-        nc.vector.tensor_tensor(
-            s_pair_all[:], e_all[:, :, : 2 * NODES], e_all[:, :, 2 * NODES :], ADD
-        )
+            nc.vector.tensor_tensor(
+                s_pair_all[:, blocks, :], e[:, :, : 2 * NODES], e[:, :, 2 * NODES :], ADD
+            )
+
         s_all = held.tile([P, BLOCKS, NODES], F32, name="s_all")
         nc.vector.tensor_tensor(s_all[:], s_pair_all[:, :, :NODES], s_pair_all[:, :, NODES:], ADD)
 

@@ -63,14 +63,15 @@ def tile_tensorcircuit_kernel(tc, base, left, right, logw, offs, out):
             nc.vector.tensor_tensor(m, m_pair[:, :, :NODES], m_pair[:, :, NODES:], MAX)
 
             shifted = held.tile([P, GROUP, ELEMENTS], F32, name=f"shifted{g}")
-            nc.vector.tensor_tensor(
-                shifted[:].rearrange("p k (a j) -> p k a j", a=CHILDREN),
-                t[:].rearrange("p k (a j) -> p k a j", a=CHILDREN),
-                m.unsqueeze(2).to_broadcast([P, GROUP, CHILDREN, NODES]),
-                SUBTRACT,
-            )
             e = held.tile([P, GROUP, ELEMENTS], F32, name=f"e{g}")
-            nc.scalar.activation(e[:], shifted[:], EXP)
+            for k in range(GROUP):
+                nc.vector.tensor_tensor(
+                    shifted[:, k, :].rearrange("p (a j) -> p a j", a=CHILDREN),
+                    t[:, k, :].rearrange("p (a j) -> p a j", a=CHILDREN),
+                    m_all[:, g * GROUP + k, :].unsqueeze(1).to_broadcast([P, CHILDREN, NODES]),
+                    SUBTRACT,
+                )
+                nc.scalar.activation(e[:, k, :], shifted[:, k, :], EXP)
 
             nc.vector.tensor_tensor(
                 s_pair_all[:, blocks, :], e[:, :, : 2 * NODES], e[:, :, 2 * NODES :], ADD

@@ -86,4 +86,5 @@ def tile_tensorcircuit_kernel(tc, base, left, right, logw, offs, out):
             nc.vector.tensor_tensor(
                 windows[k][:].indirect(offsets[:]), m_all[:, k, :], log_s[:], ADD
             )
-            nc.sync.dma_start(out_blocks[k], windows[k][:])
+            store_queue = nc.sync if k % 2 == 0 else nc.scalar
+            store_queue.dma_start(out_blocks[k], windows[k][:])

@@ -1,12 +1,14 @@
+import math
+
 import concourse.mybir as mybir
 
 F32 = mybir.dt.float32
 U16 = mybir.dt.uint16
 ADD = mybir.AluOpType.add
 SUBTRACT = mybir.AluOpType.subtract
+MULT = mybir.AluOpType.mult
 MAX = mybir.AluOpType.max
 EXP = mybir.ActivationFunctionType.Exp
-LN = mybir.ActivationFunctionType.Ln
 
 P = 128
 SAMPLES = 512
@@ -15,6 +17,10 @@ NODES = 64
 CHILDREN = 4
 ELEMENTS = CHILDREN * NODES
 BLOCKS = SAMPLES // P
+
+POINTS = (0.188359695, 1.08020636, 3.21480279)
+WEIGHTS = (2.61360835, 1.26143398, 1.00118357)
+LOG_SUM_AT_1 = sum(w * math.exp(-x) for x, w in zip(POINTS, WEIGHTS))
 GROUP = 2
 GROUPS = BLOCKS // GROUP
 
@@ -42,11 +48,7 @@ def tile_tensorcircuit_kernel(tc, base, left, right, logw, offs, out):
         for k in range(BLOCKS):
             nc.sync.dma_start(windows[k][:], base_blocks[k])
 
-        m_all = held.tile([P, BLOCKS, NODES], F32, name="m_all")
-        s_pair_all = held.tile([P, BLOCKS, 2 * NODES], F32, name="s_pair_all")
-
         for g in range(GROUPS):
-            blocks = slice(g * GROUP, (g + 1) * GROUP)
             weighted = held.tile([P, GROUP, ELEMENTS], F32, name=f"weighted{g}")
             nc.vector.tensor_tensor(
                 weighted[:],
@@ -59,32 +61,43 @@ def tile_tensorcircuit_kernel(tc, base, left, right, logw, offs, out):
 
             m_pair = held.tile([P, GROUP, 2 * NODES], F32, name=f"m_pair{g}")
             nc.vector.tensor_tensor(m_pair[:], t[:, :, : 2 * NODES], t[:, :, 2 * NODES :], MAX)
-            m = m_all[:, blocks, :]
-            nc.vector.tensor_tensor(m, m_pair[:, :, :NODES], m_pair[:, :, NODES:], MAX)
+            m = held.tile([P, GROUP, NODES], F32, name=f"m{g}")
+            nc.vector.tensor_tensor(m[:], m_pair[:, :, :NODES], m_pair[:, :, NODES:], MAX)
 
-            shifted = held.tile([P, GROUP, ELEMENTS], F32, name=f"shifted{g}")
-            e = held.tile([P, GROUP, ELEMENTS], F32, name=f"e{g}")
-            for k in range(GROUP):
+            for b in range(GROUP):
+                k = g * GROUP + b
+                shifted = held.tile([P, ELEMENTS], F32, name=f"shifted{k}")
                 nc.vector.tensor_tensor(
-                    shifted[:, k, :].rearrange("p (a j) -> p a j", a=CHILDREN),
-                    t[:, k, :].rearrange("p (a j) -> p a j", a=CHILDREN),
-                    m_all[:, g * GROUP + k, :].unsqueeze(1).to_broadcast([P, CHILDREN, NODES]),
+                    shifted[:].rearrange("p (a j) -> p a j", a=CHILDREN),
+                    t[:, b, :].rearrange("p (a j) -> p a j", a=CHILDREN),
+                    m[:, b, :].unsqueeze(1).to_broadcast([P, CHILDREN, NODES]),
                     SUBTRACT,
                 )
-                nc.scalar.activation(e[:, k, :], shifted[:, k, :], EXP)
+                e = held.tile([P, ELEMENTS], F32, name=f"e{k}")
+                nc.scalar.activation(e[:], shifted[:], EXP)
 
-            nc.vector.tensor_tensor(
-                s_pair_all[:, blocks, :], e[:, :, : 2 * NODES], e[:, :, 2 * NODES :], ADD
-            )
+                s_pair = held.tile([P, 2 * NODES], F32, name=f"s_pair{k}")
+                nc.vector.tensor_tensor(s_pair[:], e[:, : 2 * NODES], e[:, 2 * NODES :], ADD)
+                s = held.tile([P, NODES], F32, name=f"s{k}")
+                nc.vector.tensor_tensor(s[:], s_pair[:, :NODES], s_pair[:, NODES:], ADD)
 
-        s_all = held.tile([P, BLOCKS, NODES], F32, name="s_all")
-        nc.vector.tensor_tensor(s_all[:], s_pair_all[:, :, :NODES], s_pair_all[:, :, NODES:], ADD)
+                terms = []
+                for i in range(3):
+                    term = held.tile([P, NODES], F32, name=f"term{k}_{i}")
+                    nc.scalar.activation(
+                        term[:], s[:], EXP, scale=-POINTS[i], bias=math.log(WEIGHTS[i])
+                    )
+                    terms.append(term)
+                minus_two = held.tile([P, NODES], F32, name=f"minus_two{k}")
+                nc.vector.scalar_tensor_tensor(
+                    minus_two[:], terms[0][:], -1.0, terms[1][:], MULT, SUBTRACT
+                )
+                log_s = held.tile([P, NODES], F32, name=f"log_s{k}")
+                nc.vector.scalar_tensor_tensor(
+                    log_s[:], minus_two[:], LOG_SUM_AT_1, terms[2][:], ADD, SUBTRACT
+                )
 
-        for k in range(BLOCKS):
-            log_s = held.tile([P, NODES], F32, name=f"log_s{k}")
-            nc.scalar.activation(log_s[:], s_all[:, k, :], LN)
-            nc.vector.tensor_tensor(
-                windows[k][:].indirect(offsets[:]), m_all[:, k, :], log_s[:], ADD
-            )
-            store_queue = nc.sync if k % 2 == 0 else nc.scalar
-            store_queue.dma_start(out_blocks[k], windows[k][:])
+                nc.vector.tensor_tensor(
+                    windows[k][:].indirect(offsets[:]), m[:, b, :], log_s[:], ADD
+                )
+                nc.sync.dma_start(out_blocks[k], windows[k][:])

@@ -39,7 +39,7 @@ def tile_tensorcircuit_kernel(tc, base, left, right, logw, offs, out):
         logw_all = held.tile([P, ELEMENTS], F32, name="logw_all")
         offsets = held.tile([P, NODES // 16], U16, name="offsets")
 
-        nc.sync.dma_start(logw_all[:], logw.to_broadcast([P, ELEMENTS]))
+        nc.scalar.dma_start(logw_all[:], logw.to_broadcast([P, ELEMENTS]))
         for g in range(GROUPS):
             nc.sync.dma_start(rights[g][:], right_blocks[:, g * GROUP : (g + 1) * GROUP, :])
         for g in range(GROUPS):

import math

import concourse.mybir as mybir

F32 = mybir.dt.float32
U16 = mybir.dt.uint16
ADD = mybir.AluOpType.add
SUBTRACT = mybir.AluOpType.subtract
MULT = mybir.AluOpType.mult
MAX = mybir.AluOpType.max
EXP = mybir.ActivationFunctionType.Exp

P = 128
SAMPLES = 512
PLACES = 512
NODES = 64
CHILDREN = 4
ELEMENTS = CHILDREN * NODES
BLOCKS = SAMPLES // P

POINTS = (0.188359695, 1.08020636, 3.21480279)
WEIGHTS = (2.61360835, 1.26143398, 1.00118357)
LOG_SUM_AT_1 = sum(w * math.exp(-x) for x, w in zip(POINTS, WEIGHTS))
GROUP = 2
GROUPS = BLOCKS // GROUP


def tile_tensorcircuit_kernel(tc, base, left, right, logw, offs, out):
    nc = tc.nc
    left_blocks = left.rearrange("(p k) d -> p k d", k=BLOCKS)
    right_blocks = right.rearrange("(p k) d -> p k d", k=BLOCKS)
    base_blocks = base.rearrange("(p k) d -> k p d", k=BLOCKS)
    out_blocks = out.rearrange("(p k) d -> k p d", k=BLOCKS)

    with tc.tile_pool(name="held", bufs=1) as held:
        lefts = [held.tile([P, GROUP, ELEMENTS], F32, name=f"left{g}") for g in range(GROUPS)]
        rights = [held.tile([P, GROUP, ELEMENTS], F32, name=f"right{g}") for g in range(GROUPS)]
        windows = [held.tile([P, PLACES], F32, name=f"window{k}") for k in range(BLOCKS)]
        logw_all = held.tile([P, ELEMENTS], F32, name="logw_all")
        offsets = held.tile([P, NODES // 16], U16, name="offsets")

        nc.scalar.dma_start(logw_all[:], logw.to_broadcast([P, ELEMENTS]))
        for g in range(GROUPS):
            nc.sync.dma_start(rights[g][:], right_blocks[:, g * GROUP : (g + 1) * GROUP, :])
        for g in range(GROUPS):
            nc.sync.dma_start(lefts[g][:], left_blocks[:, g * GROUP : (g + 1) * GROUP, :])
        nc.sync.dma_start(offsets[:], offs)
        for k in range(BLOCKS):
            nc.sync.dma_start(windows[k][:], base_blocks[k])

        for g in range(GROUPS):
            weighted = held.tile([P, GROUP, ELEMENTS], F32, name=f"weighted{g}")
            nc.vector.tensor_tensor(
                weighted[:],
                rights[g][:],
                logw_all[:].unsqueeze(1).to_broadcast([P, GROUP, ELEMENTS]),
                ADD,
            )
            t = held.tile([P, GROUP, ELEMENTS], F32, name=f"t{g}")
            nc.vector.tensor_tensor(t[:], lefts[g][:], weighted[:], ADD)

            m_pair = held.tile([P, GROUP, 2 * NODES], F32, name=f"m_pair{g}")
            nc.vector.tensor_tensor(m_pair[:], t[:, :, : 2 * NODES], t[:, :, 2 * NODES :], MAX)
            m = held.tile([P, GROUP, NODES], F32, name=f"m{g}")
            nc.vector.tensor_tensor(m[:], m_pair[:, :, :NODES], m_pair[:, :, NODES:], MAX)

            for b in range(GROUP):
                k = g * GROUP + b
                shifted = held.tile([P, ELEMENTS], F32, name=f"shifted{k}")
                nc.vector.tensor_tensor(
                    shifted[:].rearrange("p (a j) -> p a j", a=CHILDREN),
                    t[:, b, :].rearrange("p (a j) -> p a j", a=CHILDREN),
                    m[:, b, :].unsqueeze(1).to_broadcast([P, CHILDREN, NODES]),
                    SUBTRACT,
                )
                e = held.tile([P, ELEMENTS], F32, name=f"e{k}")
                nc.scalar.activation(e[:], shifted[:], EXP)

                s_pair = held.tile([P, 2 * NODES], F32, name=f"s_pair{k}")
                nc.vector.tensor_tensor(s_pair[:], e[:, : 2 * NODES], e[:, 2 * NODES :], ADD)
                s = held.tile([P, NODES], F32, name=f"s{k}")
                nc.vector.tensor_tensor(s[:], s_pair[:, :NODES], s_pair[:, NODES:], ADD)

                terms = []
                for i in range(3):
                    term = held.tile([P, NODES], F32, name=f"term{k}_{i}")
                    nc.scalar.activation(
                        term[:], s[:], EXP, scale=-POINTS[i], bias=math.log(WEIGHTS[i])
                    )
                    terms.append(term)
                minus_two = held.tile([P, NODES], F32, name=f"minus_two{k}")
                nc.vector.scalar_tensor_tensor(
                    minus_two[:], terms[0][:], -1.0, terms[1][:], MULT, SUBTRACT
                )
                log_s = held.tile([P, NODES], F32, name=f"log_s{k}")
                nc.vector.scalar_tensor_tensor(
                    log_s[:], minus_two[:], LOG_SUM_AT_1, terms[2][:], ADD, SUBTRACT
                )

                nc.vector.tensor_tensor(
                    windows[k][:].indirect(offsets[:]), m[:, b, :], log_s[:], ADD
                )
                nc.sync.dma_start(out_blocks[k], windows[k][:])
